import numpy as np
import ml_dtypes


def mxq(x, axis, fmt="e4m3"):
    dtype, down = {"e4m3": (ml_dtypes.float8_e4m3fn, 7), "e5m2": (ml_dtypes.float8_e5m2, 14)}[fmt]
    v = np.moveaxis(np.asarray(x, np.float32).astype(ml_dtypes.bfloat16).astype(np.float64), axis, -1)
    blocks = v.reshape(v.shape[:-1] + (-1, 32))
    amax = np.abs(blocks).max(-1, keepdims=True)
    byte = np.maximum(np.where(amax > 0, np.frexp(amax)[1] - 1 + 127, 0) - down, 1)
    scale = np.exp2(byte - 127.0)
    codes = (blocks / scale).astype(np.float32).astype(dtype).astype(np.float64)
    return np.moveaxis((codes * scale).reshape(v.shape), -1, axis)


WIDE = False


def mx_kscale(k):
    if not WIDE:
        return np.ones(k)
    levels = np.array([10, -10, 5, -5, 0])
    a = np.random.permutation(np.resize(levels, k // 512 * 4)).reshape(k // 512, 4)
    idx = np.arange(k)
    return np.exp2(a[idx // 512, idx % 128 // 32])


BF16 = ml_dtypes.bfloat16


def bf(x):
    return np.asarray(x, np.float32).astype(BF16)


def f64(x):
    return np.asarray(x).astype(np.float64)


E2M1 = np.array([0.0, 0.5, 1.0, 1.5, 2.0, 3.0, 4.0, 6.0, -0.0, -0.5, -1.0, -1.5, -2.0, -3.0, -4.0, -6.0])


def pack_weight(w, fmt):
    k, n = w.shape
    w = f64(bf(w)).reshape(k // 32, 32, n)
    amax = np.abs(w).max(1)
    if fmt == "e4m3":
        byte = np.frexp(amax)[1] - 1 + 127 - 7
    else:
        mant, ex = np.frexp(amax / 6.0)
        byte = np.where(mant > 0.5, ex, ex - 1) + 127
    byte = np.clip(np.where(amax > 0, byte, 1), 1, 254)
    scaled = (w * np.exp2(127.0 - byte)[:, None, :]).reshape(k, n).astype(np.float32)
    by_word = np.ascontiguousarray(scaled.reshape(k // 512, 128, 4, n).transpose(0, 1, 3, 2))
    if fmt == "e4m3":
        words = by_word.astype(ml_dtypes.float8_e4m3fn).view(np.uint8)
    else:
        c = by_word.astype(ml_dtypes.float4_e2m1fn).view(np.uint8) & 0xF
        words = c[..., 0::2] | (c[..., 1::2] << 4)
    return np.ascontiguousarray(words), np.ascontiguousarray(byte.astype(np.uint8).reshape(k // 512, 16, n))


def unpack_weight(words, scales, fmt):
    g, p, n, _ = words.shape
    if fmt == "e4m3":
        vals = np.ascontiguousarray(words).view(ml_dtypes.float8_e4m3fn).astype(np.float64)
    else:
        nib = np.empty((g, p, n, 4), np.uint8)
        nib[..., 0::2] = words & 0xF
        nib[..., 1::2] = words >> 4
        vals = E2M1[nib]
    vals = vals * np.repeat(np.exp2(scales.astype(np.float64) - 127.0), 8, axis=1)[..., None]
    return vals.transpose(0, 1, 3, 2).reshape(g * 512, n)

def pack4(w):
    words, scales = pack_weight(w, "e2m1")
    return words.reshape(words.shape[0], 128, -1), scales


def unpack4(words, scales):
    return unpack_weight(words.reshape(words.shape[0], 128, -1, 2), scales, "e2m1")


B, D, F, NB, R = 640, 128, 1024, 4, 512
C = NB * D


def silu(v):
    return v / (1.0 + np.exp(-v))


def setup_inputs():
    s, u = mx_kscale(C), mx_kscale(F)
    g0 = bf(np.random.standard_normal((B, F)) * 0.6 * u)
    w2_0_words, w2_0_scales = pack4((np.random.standard_normal((D, F)) * 0.5 / np.sqrt(F) / u).T)
    wk_rest = bf(np.random.standard_normal((B, NB, D)) * 0.3 * s.reshape(NB, D))
    fc1_w_words, fc1_w_scales = pack4((np.random.standard_normal((R, C)) * 3.0 / np.sqrt(C) / s).T)
    fc1_b = bf(np.random.standard_normal(R) * 0.5)
    fc2_w_words, fc2_w_scales = pack4((np.random.standard_normal((D, R)) * 0.5 / np.sqrt(R)).T)
    fc2_b = bf(np.random.standard_normal(D) * 0.15)
    return {"g0": g0,
            "w2_0_words": w2_0_words,
            "w2_0_scales": w2_0_scales,
            "wk_rest": wk_rest,
            "fc1_w_words": fc1_w_words,
            "fc1_w_scales": fc1_w_scales,
            "fc1_b": fc1_b,
            "fc2_w_words": fc2_w_words,
            "fc2_w_scales": fc2_w_scales,
            "fc2_b": fc2_b}


def reference(g0, w2_0_words, w2_0_scales, wk_rest, fc1_w_words, fc1_w_scales, fc1_b, fc2_w_words, fc2_w_scales, fc2_b):
    o0 = mxq(f64(g0), 1, "e4m3") @ unpack4(w2_0_words, w2_0_scales)
    concat = f64(wk_rest).reshape(B, C)
    h = silu((mxq(concat, 1, "e4m3") @ unpack4(fc1_w_words, fc1_w_scales)) + f64(fc1_b))
    proj = (mxq(h, 1, "e4m3") @ unpack4(fc2_w_words, fc2_w_scales)) + f64(fc2_b)
    diff = o0 - proj
    return np.sqrt((diff ** 2).sum(axis=1)), np.abs(diff).mean(axis=1)

@@ -1,0 +1,251 @@
+from contextlib import ExitStack
+
+import concourse.mybir as mybir
+from concourse.masks import make_identity
+
+F32 = mybir.dt.float32
+BF16 = mybir.dt.bfloat16
+I32 = mybir.dt.int32
+U32 = mybir.dt.uint32
+U8 = mybir.dt.uint8
+FP8X4 = mybir.dt.float8_e4m3fn_x4
+FP4X4 = mybir.dt.float4_e2m1fn_x4
+ACT = mybir.ActivationFunctionType
+ALU = mybir.AluOpType
+
+P = 128
+PACK = 4
+K_PASS = P * PACK
+PAIRS = K_PASS // 2
+
+B, D, F, R = 640, 128, 1024, 512
+C = 512
+ROW_TILES = B // P
+G0_PASSES = F // K_PASS
+QUADRANTS = 4
+L1_COLUMN = 32
+EARLY_TILES = 2
+BIAS2_PAD = 256
+
+FLOPS = 2 * B * (F * D + C * R + R * D)
+
+
+def tile_nnapprox_pa_s_kernel(
+    tc,
+    g0,
+    w2_0_words,
+    w2_0_scales,
+    wk_rest,
+    fc1_w_words,
+    fc1_w_scales,
+    fc1_b,
+    fc2_w_words,
+    fc2_w_scales,
+    fc2_b,
+    out_0,
+    out_1,
+):
+    nc = tc.nc
+    with ExitStack() as ctx:
+        keep = ctx.enter_context(tc.tile_pool(name="keep", bufs=1))
+        psum = ctx.enter_context(tc.psum_pool(name="psum", bufs=8))
+        ctx.enter_context(tc.manual_schedule())
+
+        def one_per_row_tile(shape, dtype, name):
+            return [
+                keep.tile(shape, dtype, name="%s%d" % (name, i), align_bytes=64)
+                for i in range(ROW_TILES)
+            ]
+
+        bias_rows = keep.tile([P, R + BIAS2_PAD], BF16)
+        nc.vector.memset(bias_rows[:], 0.0)
+        fc1_plane = keep.tile([P, R], U8, align_bytes=64)
+        fc2_plane = keep.tile([P, D], U8, align_bytes=64)
+        w2_plane = keep.tile([P, G0_PASSES * D], U8, align_bytes=64)
+        nc.vector.memset(fc1_plane[:].bitcast(I32), 0)
+        warm = keep.tile([P, 2], F32)
+        nc.vector.memset(warm[:], 0.0)
+        nc.scalar.activation(out=warm[:, 0:1], in_=warm[:, 0:1], func=ACT.Silu)
+        nc.vector.memset(fc2_plane[:].bitcast(I32), 0)
+        nc.vector.memset(w2_plane[:].bitcast(I32), 0)
+        ones = keep.tile([P, P], BF16)
+        nc.vector.memset(ones[:], 1.0)
+        sums = keep.tile([P, P], F32)
+        nc.vector.memset(sums[:], 0.0)
+
+        wk_rows = wk_rest.rearrange("(i p) n d -> i p (n d)", p=P)
+        g0_rows = g0.rearrange("(i p) k -> i p k", p=P)
+        wk_sb = one_per_row_tile([P, C], BF16, "wk_sb")
+        g0_sb = one_per_row_tile([P, F], BF16, "g0_sb")
+        fc1_words = keep.tile([P, 2 * R], U8, align_bytes=64)
+        fc2_words = keep.tile([P, 2 * D], U8, align_bytes=64)
+        w2_words = keep.tile([P, G0_PASSES * 2 * D], U8, align_bytes=64)
+
+        def load_plane(plane, scales, passes):
+            for q4 in range(QUADRANTS):
+                nc.sync.dma_start(
+                    out=plane[32 * q4 : 32 * q4 + 4, :]
+                    .bitcast(I32)
+                    .rearrange("r (g w) -> r g w", g=passes),
+                    in_=scales[:, 4 * q4 : 4 * q4 + 4, :].bitcast(I32).rearrange("g r w -> r g w"),
+                )
+
+        def load_words(words, packed, passes):
+            nc.sync.dma_start(
+                out=words[:].bitcast(I32).rearrange("p (g w) -> p g w", g=passes),
+                in_=packed.bitcast(I32).rearrange("g p w -> p g w"),
+            )
+
+        for i in range(EARLY_TILES):
+            nc.sync.dma_start(out=wk_sb[i][:], in_=wk_rows[i])
+        nc.sync.dma_start(out=bias_rows[0:1, 0:R], in_=fc1_b.rearrange("(o r) -> o r", o=1))
+        load_plane(fc1_plane, fc1_w_scales, 1)
+        load_words(fc1_words, fc1_w_words, 1)
+        for i in range(EARLY_TILES, ROW_TILES):
+            nc.sync.dma_start(out=wk_sb[i][:], in_=wk_rows[i])
+        nc.sync.dma_start(out=bias_rows[0:1, R : R + D], in_=fc2_b.rearrange("(o d) -> o d", o=1))
+        load_plane(fc2_plane, fc2_w_scales, 1)
+        load_words(fc2_words, fc2_w_words, 1)
+        load_plane(w2_plane, w2_0_scales, G0_PASSES)
+        load_words(w2_words, w2_0_words, G0_PASSES)
+        ident = keep.tile([P, P], F32)
+        make_identity(nc, ident[:])
+        for i in range(ROW_TILES):
+            nc.gpsimd.dma_start(out=g0_sb[i][:], in_=g0_rows[i])
+
+        def spread_bias(first, width, used, copy_out, spread):
+            bias_bank = psum.tile([P, width], F32, tag="bank")
+            nc.tensor.matmul(
+                out=bias_bank[:],
+                lhsT=ones[:],
+                rhs=bias_rows[:, first : first + width],
+                start=True,
+                stop=True,
+            )
+            copy_out(out=spread[:], in_=bias_bank[:, 0:used])
+
+        def turn_rows(x_sb, passes, copy_out, grouped):
+            x_pairs = x_sb[:].bitcast(F32)
+            turned = psum.tile([P, passes, 2, P], F32, tag="bank")
+            for g in range(passes):
+                for u in range(2):
+                    nc.tensor.transpose(
+                        out=turned[:, g, u, :],
+                        in_=x_pairs[:, PAIRS * g + u : PAIRS * (g + 1) : 2],
+                        identity=ident[:],
+                    )
+            copy_out(
+                out=grouped[:].bitcast(F32).rearrange("p (g b u) -> p g b u", g=passes, u=2),
+                in_=turned[:].rearrange("p g u b -> p g b u"),
+            )
+
+        def quantise(grouped, codes, plane):
+            nc.vector.quantize_mx(out=codes[:].bitcast(FP8X4), scales=plane[:], in_=grouped[:])
+
+        c_grouped = one_per_row_tile([P, PACK * P], BF16, "c_grouped")
+        c_codes = one_per_row_tile([P, P], U32, "c_codes")
+        c_plane = one_per_row_tile([P, P], U8, "c_plane")
+        h_grouped = one_per_row_tile([P, PACK * P], BF16, "h_grouped")
+        h_codes = one_per_row_tile([P, P], U32, "h_codes")
+        h_plane = one_per_row_tile([P, P], U8, "h_plane")
+        g_grouped = one_per_row_tile([P, G0_PASSES * PACK * P], BF16, "g_grouped")
+        g_codes = one_per_row_tile([P, G0_PASSES * P], U32, "g_codes")
+        g_plane = one_per_row_tile([P, G0_PASSES * P], U8, "g_plane")
+        pre = one_per_row_tile([P, R], F32, "pre")
+        h_sb = one_per_row_tile([P, R], BF16, "h_sb")
+        o0_less_b2 = one_per_row_tile([P, D], F32, "o0_less_b2")
+        diff = one_per_row_tile([P, D], F32, "diff")
+        squares = one_per_row_tile([P, D], F32, "squares")
+        sizes = one_per_row_tile([P, D], F32, "sizes")
+
+        b1_all = keep.tile([P, R], F32)
+        for i in range(EARLY_TILES):
+            turn_rows(wk_sb[i], 1, nc.scalar.copy, c_grouped[i])
+            quantise(c_grouped[i], c_codes[i], c_plane[i])
+        spread_bias(0, R, R, nc.vector.tensor_copy, b1_all)
+        for i in range(EARLY_TILES, ROW_TILES):
+            turn_rows(wk_sb[i], 1, nc.scalar.copy, c_grouped[i])
+            quantise(c_grouped[i], c_codes[i], c_plane[i])
+
+        for i in range(ROW_TILES):
+            fc1_bank = psum.tile([P, R], F32, tag="bank")
+            nc.tensor.matmul_mx(
+                out=fc1_bank[:],
+                lhsT=c_codes[i][:].bitcast(FP8X4),
+                lhsT_scale=c_plane[i][:],
+                rhs=fc1_words[:].bitcast(FP4X4),
+                rhs_scale=fc1_plane[:],
+                start=True,
+                stop=True,
+            )
+            nc.vector.tensor_tensor(out=pre[i][:], in0=fc1_bank[:], in1=b1_all[:], op=ALU.add)
+            nc.scalar.activation(out=h_sb[i][:], in_=pre[i][:], func=ACT.Silu)
+
+        b2_all = keep.tile([P, D], F32)
+        spread_bias(R, BIAS2_PAD, D, nc.scalar.copy, b2_all)
+        for i in range(ROW_TILES):
+            turn_rows(h_sb[i], 1, nc.vector.tensor_copy, h_grouped[i])
+            turn_rows(g0_sb[i], G0_PASSES, nc.scalar.copy, g_grouped[i])
+            if i > 0:
+                quantise(g_grouped[i - 1], g_codes[i - 1], g_plane[i - 1])
+            quantise(h_grouped[i], h_codes[i], h_plane[i])
+        quantise(g_grouped[ROW_TILES - 1], g_codes[ROW_TILES - 1], g_plane[ROW_TILES - 1])
+        nc.scalar.activation(out=warm[:, 1:2], in_=warm[:, 1:2], func=ACT.Sqrt)
+
+        for i in range(ROW_TILES):
+            o0_bank = psum.tile([P, D], F32, tag="bank")
+            for g in range(G0_PASSES):
+                nc.tensor.matmul_mx(
+                    out=o0_bank[:],
+                    lhsT=g_codes[i][:, P * g : P * (g + 1)].bitcast(FP8X4),
+                    lhsT_scale=g_plane[i][:, P * g : P * (g + 1)],
+                    rhs=w2_words[:, 2 * D * g : 2 * D * (g + 1)].bitcast(FP4X4),
+                    rhs_scale=w2_plane[:, D * g : D * (g + 1)],
+                    start=(g == 0),
+                    stop=(g == G0_PASSES - 1),
+                )
+            nc.vector.tensor_tensor(
+                out=o0_less_b2[i][:], in0=o0_bank[:], in1=b2_all[:], op=ALU.subtract
+            )
+
+        for i in range(ROW_TILES):
+            proj_bank = psum.tile([P, D], F32, tag="bank")
+            nc.tensor.matmul_mx(
+                out=proj_bank[:],
+                lhsT=h_codes[i][:].bitcast(FP8X4),
+                lhsT_scale=h_plane[i][:],
+                rhs=fc2_words[:].bitcast(FP4X4),
+                rhs_scale=fc2_plane[:],
+                start=True,
+                stop=True,
+            )
+            nc.vector.tensor_tensor(
+                out=diff[i][:], in0=o0_less_b2[i][:], in1=proj_bank[:], op=ALU.subtract
+            )
+            nc.scalar.activation(
+                out=squares[i][:], in_=diff[i][:], func=ACT.Square, accum_out=sums[:, i : i + 1]
+            )
+            nc.scalar.activation(
+                out=sizes[i][:],
+                in_=diff[i][:],
+                func=ACT.Abs,
+                scale=1.0 / D,
+                accum_out=sums[:, L1_COLUMN + i : L1_COLUMN + i + 1],
+            )
+
+        sums_bank = psum.tile([P, P], F32, tag="bank")
+        nc.tensor.transpose(out=sums_bank[:], in_=sums[:], identity=ident[:])
+        l2_rows = keep.tile([P, P], F32)
+        l1_rows = keep.tile([P, P], F32)
+        nc.scalar.activation(
+            out=l2_rows[0:ROW_TILES, :], in_=sums_bank[0:ROW_TILES, :], func=ACT.Sqrt
+        )
+        nc.vector.tensor_copy(
+            out=l1_rows[L1_COLUMN : L1_COLUMN + ROW_TILES, :],
+            in_=sums_bank[L1_COLUMN : L1_COLUMN + ROW_TILES, :],
+        )
+        nc.sync.dma_start(out=out_0.rearrange("(i p) -> i p", p=P), in_=l2_rows[0:ROW_TILES, :])
+        nc.sync.dma_start(
+            out=out_1.rearrange("(i p) -> i p", p=P),
+            in_=l1_rows[L1_COLUMN : L1_COLUMN + ROW_TILES, :],
+        )

@@ -23,9 +23,6 @@ C = 512
 ROW_TILES = B // P
 G0_PASSES = F // K_PASS
 QUADRANTS = 4
-L1_COLUMN = 32
-EARLY_TILES = 2
-BIAS2_PAD = 256
 
 FLOPS = 2 * B * (F * D + C * R + R * D)
 
@@ -57,29 +54,32 @@ def tile_nnapprox_pa_s_kernel(
                 for i in range(ROW_TILES)
             ]
 
-        bias_rows = keep.tile([P, R + BIAS2_PAD], BF16)
-        nc.vector.memset(bias_rows[:], 0.0)
-        fc1_plane = keep.tile([P, R], U8, align_bytes=64)
+        fc1_plane_in = keep.tile([P, R], U8, align_bytes=64)
         fc2_plane = keep.tile([P, D], U8, align_bytes=64)
         w2_plane = keep.tile([P, G0_PASSES * D], U8, align_bytes=64)
-        nc.vector.memset(fc1_plane[:].bitcast(I32), 0)
+        bias2_rows = keep.tile([P, D], BF16)
+        nc.vector.memset(fc1_plane_in[:].bitcast(I32), 0)
         warm = keep.tile([P, 2], F32)
         nc.vector.memset(warm[:], 0.0)
         nc.scalar.activation(out=warm[:, 0:1], in_=warm[:, 0:1], func=ACT.Silu)
+        nc.vector.memset(bias2_rows[:], 0.0)
         nc.vector.memset(fc2_plane[:].bitcast(I32), 0)
         nc.vector.memset(w2_plane[:].bitcast(I32), 0)
         ones = keep.tile([P, P], BF16)
         nc.vector.memset(ones[:], 1.0)
-        sums = keep.tile([P, P], F32)
-        nc.vector.memset(sums[:], 0.0)
+        square_sums = keep.tile([P, P], F32)
+        nc.vector.memset(square_sums[:], 0.0)
+        size_sums = keep.tile([P, P], F32)
+        nc.vector.memset(size_sums[:], 0.0)
 
-        wk_rows = wk_rest.rearrange("(i p) n d -> i p (n d)", p=P)
-        g0_rows = g0.rearrange("(i p) k -> i p k", p=P)
-        wk_sb = one_per_row_tile([P, C], BF16, "wk_sb")
-        g0_sb = one_per_row_tile([P, F], BF16, "g0_sb")
-        fc1_words = keep.tile([P, 2 * R], U8, align_bytes=64)
+        wk_rows = wk_rest.rearrange("(i p) n d -> p i (n d)", p=P)
+        g0_rows = g0.rearrange("(i p) k -> p i k", p=P)
+        wk_sb = keep.tile([P, ROW_TILES, C], BF16, align_bytes=64)
+        g0_sb = keep.tile([P, ROW_TILES, F], BF16, align_bytes=64)
+        fc1_words_in = keep.tile([P, 2 * R], U8, align_bytes=64)
         fc2_words = keep.tile([P, 2 * D], U8, align_bytes=64)
         w2_words = keep.tile([P, G0_PASSES * 2 * D], U8, align_bytes=64)
+        bias1 = keep.tile([P, PACK], BF16)
 
         def load_plane(plane, scales, passes):
             for q4 in range(QUADRANTS):
@@ -96,36 +96,54 @@ def tile_nnapprox_pa_s_kernel(
                 in_=packed.bitcast(I32).rearrange("g p w -> p g w"),
             )
 
-        for i in range(EARLY_TILES):
-            nc.sync.dma_start(out=wk_sb[i][:], in_=wk_rows[i])
-        nc.sync.dma_start(out=bias_rows[0:1, 0:R], in_=fc1_b.rearrange("(o r) -> o r", o=1))
-        load_plane(fc1_plane, fc1_w_scales, 1)
-        load_words(fc1_words, fc1_w_words, 1)
-        for i in range(EARLY_TILES, ROW_TILES):
-            nc.sync.dma_start(out=wk_sb[i][:], in_=wk_rows[i])
-        nc.sync.dma_start(out=bias_rows[0:1, R : R + D], in_=fc2_b.rearrange("(o d) -> o d", o=1))
-        load_plane(fc2_plane, fc2_w_scales, 1)
-        load_words(fc2_words, fc2_w_words, 1)
+        def load_rows(queue, x_sb, x_rows, first, end):
+            queue.dma_start(out=x_sb[:, first:end, :], in_=x_rows[:, first:end, :])
+
+        load_rows(nc.sync, wk_sb, wk_rows, 0, 1)
+        load_plane(fc1_plane_in, fc1_w_scales, 1)
+        load_words(fc1_words_in, fc1_w_words, 1)
+        nc.sync.dma_start(out=bias1[:], in_=fc1_b.rearrange("(p t) -> p t", t=PACK))
+        load_rows(nc.sync, wk_sb, wk_rows, 1, 3)
+        load_rows(nc.sync, wk_sb, wk_rows, 3, 5)
+        load_rows(nc.sync, g0_sb, g0_rows, 0, 1)
+        nc.sync.dma_start(out=bias2_rows[0:1, :], in_=fc2_b.rearrange("(o d) -> o d", o=1))
+        load_rows(nc.sync, g0_sb, g0_rows, 1, 3)
+        load_rows(nc.sync, g0_sb, g0_rows, 3, 5)
         load_plane(w2_plane, w2_0_scales, G0_PASSES)
         load_words(w2_words, w2_0_words, G0_PASSES)
+        load_plane(fc2_plane, fc2_w_scales, 1)
+        load_words(fc2_words, fc2_w_words, 1)
         ident = keep.tile([P, P], F32)
         make_identity(nc, ident[:])
-        for i in range(ROW_TILES):
-            nc.gpsimd.dma_start(out=g0_sb[i][:], in_=g0_rows[i])
 
-        def spread_bias(first, width, used, copy_out, spread):
-            bias_bank = psum.tile([P, width], F32, tag="bank")
-            nc.tensor.matmul(
-                out=bias_bank[:],
-                lhsT=ones[:],
-                rhs=bias_rows[:, first : first + width],
-                start=True,
-                stop=True,
-            )
-            copy_out(out=spread[:], in_=bias_bank[:, 0:used])
+        fc1_words = keep.tile([P, 2 * R], U8, align_bytes=64)
+        fc1_plane = keep.tile([P, R], U8, align_bytes=64)
+        nc.vector.tensor_copy(
+            out=fc1_plane[:].rearrange("p (t m) -> p t m", t=PACK),
+            in_=fc1_plane_in[:].rearrange("p (m t) -> p t m", t=PACK),
+        )
+        nc.vector.tensor_copy(
+            out=fc1_words[:].rearrange("p (t m e) -> p t m e", t=PACK, e=2),
+            in_=fc1_words_in[:].rearrange("p (m t e) -> p t m e", t=PACK, e=2),
+        )
 
-        def turn_rows(x_sb, passes, copy_out, grouped):
-            x_pairs = x_sb[:].bitcast(F32)
+        c_grouped = one_per_row_tile([P, PACK * P], BF16, "c_grouped")
+        c_codes = one_per_row_tile([P, P], U32, "c_codes")
+        c_plane = one_per_row_tile([P, P], U8, "c_plane")
+        h_sb = one_per_row_tile([P, PACK, P], BF16, "h_sb")
+        h_grouped = one_per_row_tile([P, PACK * P], BF16, "h_grouped")
+        h_codes = one_per_row_tile([P, P], U32, "h_codes")
+        h_plane = one_per_row_tile([P, P], U8, "h_plane")
+        g_grouped = one_per_row_tile([P, G0_PASSES * PACK * P], BF16, "g_grouped")
+        g_codes = one_per_row_tile([P, G0_PASSES * P], U32, "g_codes")
+        g_plane = one_per_row_tile([P, G0_PASSES * P], U8, "g_plane")
+        diff = one_per_row_tile([P, D], F32, "diff")
+        squares = one_per_row_tile([P, D], F32, "squares")
+        sizes = one_per_row_tile([P, D], F32, "sizes")
+        banks = {}
+
+        def turn_rows(x, passes, key):
+            x_pairs = x.bitcast(F32)
             turned = psum.tile([P, passes, 2, P], F32, tag="bank")
             for g in range(passes):
                 for u in range(2):
@@ -134,118 +152,197 @@ def tile_nnapprox_pa_s_kernel(
                         in_=x_pairs[:, PAIRS * g + u : PAIRS * (g + 1) : 2],
                         identity=ident[:],
                     )
+            banks[key] = turned
+
+        def group_rows(copy_out, key, passes, grouped):
             copy_out(
                 out=grouped[:].bitcast(F32).rearrange("p (g b u) -> p g b u", g=passes, u=2),
-                in_=turned[:].rearrange("p g u b -> p g b u"),
+                in_=banks[key][:].rearrange("p g u b -> p g b u"),
             )
 
         def quantise(grouped, codes, plane):
             nc.vector.quantize_mx(out=codes[:].bitcast(FP8X4), scales=plane[:], in_=grouped[:])
 
-        c_grouped = one_per_row_tile([P, PACK * P], BF16, "c_grouped")
-        c_codes = one_per_row_tile([P, P], U32, "c_codes")
-        c_plane = one_per_row_tile([P, P], U8, "c_plane")
-        h_grouped = one_per_row_tile([P, PACK * P], BF16, "h_grouped")
-        h_codes = one_per_row_tile([P, P], U32, "h_codes")
-        h_plane = one_per_row_tile([P, P], U8, "h_plane")
-        g_grouped = one_per_row_tile([P, G0_PASSES * PACK * P], BF16, "g_grouped")
-        g_codes = one_per_row_tile([P, G0_PASSES * P], U32, "g_codes")
-        g_plane = one_per_row_tile([P, G0_PASSES * P], U8, "g_plane")
-        pre = one_per_row_tile([P, R], F32, "pre")
-        h_sb = one_per_row_tile([P, R], BF16, "h_sb")
-        o0_less_b2 = one_per_row_tile([P, D], F32, "o0_less_b2")
-        diff = one_per_row_tile([P, D], F32, "diff")
-        squares = one_per_row_tile([P, D], F32, "squares")
-        sizes = one_per_row_tile([P, D], F32, "sizes")
+        def turn_c(i):
+            turn_rows(wk_sb[:, i, :], 1, ("c", i))
 
-        b1_all = keep.tile([P, R], F32)
-        for i in range(EARLY_TILES):
-            turn_rows(wk_sb[i], 1, nc.scalar.copy, c_grouped[i])
-            quantise(c_grouped[i], c_codes[i], c_plane[i])
-        spread_bias(0, R, R, nc.vector.tensor_copy, b1_all)
-        for i in range(EARLY_TILES, ROW_TILES):
-            turn_rows(wk_sb[i], 1, nc.scalar.copy, c_grouped[i])
+        def copy_c(i, copy_out):
+            group_rows(copy_out, ("c", i), 1, c_grouped[i])
+
+        def quantise_c(i):
             quantise(c_grouped[i], c_codes[i], c_plane[i])
 
-        for i in range(ROW_TILES):
-            fc1_bank = psum.tile([P, R], F32, tag="bank")
-            nc.tensor.matmul_mx(
-                out=fc1_bank[:],
-                lhsT=c_codes[i][:].bitcast(FP8X4),
-                lhsT_scale=c_plane[i][:],
-                rhs=fc1_words[:].bitcast(FP4X4),
-                rhs_scale=fc1_plane[:],
-                start=True,
-                stop=True,
+        def multiply_c(i):
+            h_bank = psum.tile([P, PACK, P], F32, tag="bank")
+            for t in range(PACK):
+                nc.tensor.matmul_mx(
+                    out=h_bank[:, t, :],
+                    lhsT=fc1_words[:, 2 * P * t : 2 * P * (t + 1)].bitcast(FP4X4),
+                    lhsT_scale=fc1_plane[:, P * t : P * (t + 1)],
+                    rhs=c_codes[i][:].bitcast(FP8X4),
+                    rhs_scale=c_plane[i][:],
+                    start=True,
+                    stop=True,
+                )
+            banks[("h", i)] = h_bank
+
+        def silu(i):
+            for t in range(PACK):
+                nc.scalar.activation(
+                    out=h_sb[i][:, t, :],
+                    in_=banks[("h", i)][:, t, :],
+                    func=ACT.Silu,
+                    bias=bias1[:, t : t + 1],
+                )
+
+        def group_h(i):
+            nc.vector.tensor_scalar_mul(
+                out=h_grouped[i][:].rearrange("p (b t) -> p b t", t=PACK),
+                in0=h_sb[i][:].rearrange("p t b -> p b t"),
+                scalar1=-1.0,
             )
-            nc.vector.tensor_tensor(out=pre[i][:], in0=fc1_bank[:], in1=b1_all[:], op=ALU.add)
-            nc.scalar.activation(out=h_sb[i][:], in_=pre[i][:], func=ACT.Silu)
 
-        b2_all = keep.tile([P, D], F32)
-        spread_bias(R, BIAS2_PAD, D, nc.scalar.copy, b2_all)
-        for i in range(ROW_TILES):
-            turn_rows(h_sb[i], 1, nc.vector.tensor_copy, h_grouped[i])
-            turn_rows(g0_sb[i], G0_PASSES, nc.scalar.copy, g_grouped[i])
-            if i > 0:
-                quantise(g_grouped[i - 1], g_codes[i - 1], g_plane[i - 1])
+        def quantise_h(i):
             quantise(h_grouped[i], h_codes[i], h_plane[i])
-        quantise(g_grouped[ROW_TILES - 1], g_codes[ROW_TILES - 1], g_plane[ROW_TILES - 1])
-        nc.scalar.activation(out=warm[:, 1:2], in_=warm[:, 1:2], func=ACT.Sqrt)
 
-        for i in range(ROW_TILES):
-            o0_bank = psum.tile([P, D], F32, tag="bank")
+        def turn_g(i):
+            turn_rows(g0_sb[:, i, :], G0_PASSES, ("g", i))
+
+        def copy_g(i, copy_out):
+            group_rows(copy_out, ("g", i), G0_PASSES, g_grouped[i])
+
+        def quantise_g(i):
+            quantise(g_grouped[i], g_codes[i], g_plane[i])
+
+        def multiply_out(i):
+            out_bank = psum.tile([P, D], F32, tag="bank")
             for g in range(G0_PASSES):
                 nc.tensor.matmul_mx(
-                    out=o0_bank[:],
+                    out=out_bank[:],
                     lhsT=g_codes[i][:, P * g : P * (g + 1)].bitcast(FP8X4),
                     lhsT_scale=g_plane[i][:, P * g : P * (g + 1)],
                     rhs=w2_words[:, 2 * D * g : 2 * D * (g + 1)].bitcast(FP4X4),
                     rhs_scale=w2_plane[:, D * g : D * (g + 1)],
                     start=(g == 0),
-                    stop=(g == G0_PASSES - 1),
+                    stop=False,
                 )
-            nc.vector.tensor_tensor(
-                out=o0_less_b2[i][:], in0=o0_bank[:], in1=b2_all[:], op=ALU.subtract
-            )
-
-        for i in range(ROW_TILES):
-            proj_bank = psum.tile([P, D], F32, tag="bank")
             nc.tensor.matmul_mx(
-                out=proj_bank[:],
+                out=out_bank[:],
                 lhsT=h_codes[i][:].bitcast(FP8X4),
                 lhsT_scale=h_plane[i][:],
                 rhs=fc2_words[:].bitcast(FP4X4),
                 rhs_scale=fc2_plane[:],
-                start=True,
+                start=False,
                 stop=True,
             )
+            banks[("out", i)] = out_bank
+
+        def subtract_bias(i):
             nc.vector.tensor_tensor(
-                out=diff[i][:], in0=o0_less_b2[i][:], in1=proj_bank[:], op=ALU.subtract
+                out=diff[i][:], in0=banks[("out", i)][:], in1=bias2[:], op=ALU.subtract
             )
+
+        def sum_squares(i):
             nc.scalar.activation(
-                out=squares[i][:], in_=diff[i][:], func=ACT.Square, accum_out=sums[:, i : i + 1]
+                out=squares[i][:], in_=diff[i][:], func=ACT.Square, accum_out=square_sums[:, i : i + 1]
             )
+
+        def sum_sizes(i):
             nc.scalar.activation(
                 out=sizes[i][:],
                 in_=diff[i][:],
                 func=ACT.Abs,
                 scale=1.0 / D,
-                accum_out=sums[:, L1_COLUMN + i : L1_COLUMN + i + 1],
+                accum_out=size_sums[:, i : i + 1],
             )
 
-        sums_bank = psum.tile([P, P], F32, tag="bank")
-        nc.tensor.transpose(out=sums_bank[:], in_=sums[:], identity=ident[:])
-        l2_rows = keep.tile([P, P], F32)
+        turn_c(0)
+        copy_c(0, nc.scalar.copy)
+        quantise_c(0)
+        turn_c(1)
+        copy_c(1, nc.scalar.copy)
+        turn_c(2)
+        copy_c(2, nc.scalar.copy)
+        quantise_c(1)
+        multiply_c(0)
+        silu(0)
+        turn_c(3)
+        copy_c(3, nc.scalar.copy)
+        quantise_c(2)
+        turn_c(4)
+        copy_c(4, nc.vector.tensor_copy)
+        multiply_c(1)
+        quantise_c(3)
+        group_h(0)
+        quantise_c(4)
+        silu(1)
+        turn_g(0)
+        copy_g(0, nc.scalar.copy)
+        multiply_c(2)
+        quantise_h(0)
+        group_h(1)
+        silu(2)
+        multiply_c(3)
+        quantise_g(0)
+        quantise_h(1)
+        group_h(2)
+        silu(3)
+        turn_g(1)
+        copy_g(1, nc.vector.tensor_copy)
+        multiply_c(4)
+        silu(4)
+        nc.scalar.activation(out=warm[:, 1:2], in_=warm[:, 1:2], func=ACT.Sqrt)
+        bias2 = keep.tile([P, D], F32)
+        bias2_bank = psum.tile([P, D], F32, tag="bank")
+        nc.tensor.matmul(
+            out=bias2_bank[:], lhsT=ones[:], rhs=bias2_rows[:], start=True, stop=True
+        )
+        nc.vector.tensor_copy(out=bias2[:], in_=bias2_bank[:])
+        quantise_h(2)
+        group_h(3)
+        quantise_g(1)
+        turn_g(2)
+        copy_g(2, nc.scalar.copy)
+        multiply_out(0)
+        quantise_h(3)
+        group_h(4)
+        subtract_bias(0)
+        turn_g(3)
+        copy_g(3, nc.vector.tensor_copy)
+        sum_squares(0)
+        sum_sizes(0)
+        quantise_g(2)
+        quantise_h(4)
+        multiply_out(1)
+        subtract_bias(1)
+        turn_g(4)
+        quantise_g(3)
+        copy_g(4, nc.scalar.copy)
+        multiply_out(2)
+        subtract_bias(2)
+        multiply_out(3)
+        sum_squares(1)
+        sum_sizes(1)
+        quantise_g(4)
+        subtract_bias(3)
+        sum_squares(2)
+        sum_sizes(2)
+        multiply_out(4)
+        subtract_bias(4)
+        sum_squares(3)
+        sum_sizes(3)
+        sum_sizes(4)
+        sum_squares(4)
+
+        size_bank = psum.tile([P, P], F32, tag="bank")
+        nc.tensor.transpose(out=size_bank[:], in_=size_sums[:], identity=ident[:])
+        square_bank = psum.tile([P, P], F32, tag="bank")
+        nc.tensor.transpose(out=square_bank[:], in_=square_sums[:], identity=ident[:])
         l1_rows = keep.tile([P, P], F32)
+        l2_rows = keep.tile([P, P], F32)
+        nc.vector.tensor_copy(out=l1_rows[0:ROW_TILES, :], in_=size_bank[0:ROW_TILES, :])
         nc.scalar.activation(
-            out=l2_rows[0:ROW_TILES, :], in_=sums_bank[0:ROW_TILES, :], func=ACT.Sqrt
+            out=l2_rows[0:ROW_TILES, :], in_=square_bank[0:ROW_TILES, :], func=ACT.Sqrt
         )
-        nc.vector.tensor_copy(
-            out=l1_rows[L1_COLUMN : L1_COLUMN + ROW_TILES, :],
-            in_=sums_bank[L1_COLUMN : L1_COLUMN + ROW_TILES, :],
-        )
+        nc.sync.dma_start(out=out_1.rearrange("(i p) -> i p", p=P), in_=l1_rows[0:ROW_TILES, :])
         nc.sync.dma_start(out=out_0.rearrange("(i p) -> i p", p=P), in_=l2_rows[0:ROW_TILES, :])
-        nc.sync.dma_start(
-            out=out_1.rearrange("(i p) -> i p", p=P),
-            in_=l1_rows[L1_COLUMN : L1_COLUMN + ROW_TILES, :],
-        )

@@ -99,12 +99,12 @@ def tile_nnapprox_pa_s_kernel(
         def load_rows(queue, x_sb, x_rows, first, end):
             queue.dma_start(out=x_sb[:, first:end, :], in_=x_rows[:, first:end, :])
 
-        load_rows(nc.sync, wk_sb, wk_rows, 0, 1)
         load_plane(fc1_plane_in, fc1_w_scales, 1)
-        load_words(fc1_words_in, fc1_w_words, 1)
-        nc.sync.dma_start(out=bias1[:], in_=fc1_b.rearrange("(p t) -> p t", t=PACK))
+        load_rows(nc.sync, wk_sb, wk_rows, 0, 1)
         load_rows(nc.sync, wk_sb, wk_rows, 1, 3)
+        load_words(fc1_words_in, fc1_w_words, 1)
         load_rows(nc.sync, wk_sb, wk_rows, 3, 5)
+        nc.sync.dma_start(out=bias1[:], in_=fc1_b.rearrange("(p t) -> p t", t=PACK))
         load_rows(nc.sync, g0_sb, g0_rows, 0, 1)
         nc.sync.dma_start(out=bias2_rows[0:1, :], in_=fc2_b.rearrange("(o d) -> o d", o=1))
         load_rows(nc.sync, g0_sb, g0_rows, 1, 3)
@@ -118,15 +118,6 @@ def tile_nnapprox_pa_s_kernel(
 
         fc1_words = keep.tile([P, 2 * R], U8, align_bytes=64)
         fc1_plane = keep.tile([P, R], U8, align_bytes=64)
-        nc.vector.tensor_copy(
-            out=fc1_plane[:].rearrange("p (t m) -> p t m", t=PACK),
-            in_=fc1_plane_in[:].rearrange("p (m t) -> p t m", t=PACK),
-        )
-        nc.vector.tensor_copy(
-            out=fc1_words[:].rearrange("p (t m e) -> p t m e", t=PACK, e=2),
-            in_=fc1_words_in[:].rearrange("p (m t e) -> p t m e", t=PACK, e=2),
-        )
-
         c_grouped = one_per_row_tile([P, PACK * P], BF16, "c_grouped")
         c_codes = one_per_row_tile([P, P], U32, "c_codes")
         c_plane = one_per_row_tile([P, P], U8, "c_plane")
@@ -162,6 +153,16 @@ def tile_nnapprox_pa_s_kernel(
 
         def quantise(grouped, codes, plane):
             nc.vector.quantize_mx(out=codes[:].bitcast(FP8X4), scales=plane[:], in_=grouped[:])
+
+        def regroup_fc1():
+            nc.vector.tensor_copy(
+                out=fc1_plane[:].rearrange("p (t m) -> p t m", t=PACK),
+                in_=fc1_plane_in[:].rearrange("p (m t) -> p t m", t=PACK),
+            )
+            nc.vector.tensor_copy(
+                out=fc1_words[:].rearrange("p (t m e) -> p t m e", t=PACK, e=2),
+                in_=fc1_words_in[:].rearrange("p (m t e) -> p t m e", t=PACK, e=2),
+            )
 
         def turn_c(i):
             turn_rows(wk_sb[:, i, :], 1, ("c", i))
@@ -258,79 +259,80 @@ def tile_nnapprox_pa_s_kernel(
 
         turn_c(0)
         copy_c(0, nc.scalar.copy)
-        quantise_c(0)
         turn_c(1)
         copy_c(1, nc.scalar.copy)
+        quantise_c(0)
         turn_c(2)
         copy_c(2, nc.scalar.copy)
         quantise_c(1)
-        multiply_c(0)
-        silu(0)
         turn_c(3)
         copy_c(3, nc.scalar.copy)
+        regroup_fc1()
         quantise_c(2)
         turn_c(4)
-        copy_c(4, nc.vector.tensor_copy)
-        multiply_c(1)
+        copy_c(4, nc.scalar.copy)
         quantise_c(3)
-        group_h(0)
+        multiply_c(0)
+        silu(0)
         quantise_c(4)
+        multiply_c(1)
         silu(1)
-        turn_g(0)
-        copy_g(0, nc.scalar.copy)
+        group_h(0)
         multiply_c(2)
+        silu(2)
         quantise_h(0)
         group_h(1)
-        silu(2)
         multiply_c(3)
-        quantise_g(0)
+        silu(3)
         quantise_h(1)
         group_h(2)
-        silu(3)
-        turn_g(1)
-        copy_g(1, nc.vector.tensor_copy)
         multiply_c(4)
         silu(4)
+        turn_g(0)
+        copy_g(0, nc.vector.tensor_copy)
         nc.scalar.activation(out=warm[:, 1:2], in_=warm[:, 1:2], func=ACT.Sqrt)
+        quantise_h(2)
+        turn_g(1)
+        copy_g(1, nc.vector.tensor_copy)
+        group_h(3)
+        quantise_g(0)
+        turn_g(2)
+        copy_g(2, nc.scalar.copy)
+        quantise_h(3)
+        group_h(4)
+        quantise_g(1)
+        turn_g(3)
+        copy_g(3, nc.vector.tensor_copy)
+        turn_g(4)
+        copy_g(4, nc.scalar.copy)
+        quantise_h(4)
         bias2 = keep.tile([P, D], F32)
         bias2_bank = psum.tile([P, D], F32, tag="bank")
         nc.tensor.matmul(
             out=bias2_bank[:], lhsT=ones[:], rhs=bias2_rows[:], start=True, stop=True
         )
         nc.vector.tensor_copy(out=bias2[:], in_=bias2_bank[:])
-        quantise_h(2)
-        group_h(3)
-        quantise_g(1)
-        turn_g(2)
-        copy_g(2, nc.scalar.copy)
+        quantise_g(2)
         multiply_out(0)
-        quantise_h(3)
-        group_h(4)
+        quantise_g(3)
         subtract_bias(0)
-        turn_g(3)
-        copy_g(3, nc.vector.tensor_copy)
+        multiply_out(1)
         sum_squares(0)
         sum_sizes(0)
-        quantise_g(2)
-        quantise_h(4)
-        multiply_out(1)
+        quantise_g(4)
         subtract_bias(1)
-        turn_g(4)
-        quantise_g(3)
-        copy_g(4, nc.scalar.copy)
         multiply_out(2)
-        subtract_bias(2)
-        multiply_out(3)
         sum_squares(1)
         sum_sizes(1)
-        quantise_g(4)
-        subtract_bias(3)
+        subtract_bias(2)
+        multiply_out(3)
         sum_squares(2)
         sum_sizes(2)
+        subtract_bias(3)
         multiply_out(4)
-        subtract_bias(4)
         sum_squares(3)
         sum_sizes(3)
+        subtract_bias(4)
         sum_sizes(4)
         sum_squares(4)
 
@@ -344,5 +346,8 @@ def tile_nnapprox_pa_s_kernel(
         nc.scalar.activation(
             out=l2_rows[0:ROW_TILES, :], in_=square_bank[0:ROW_TILES, :], func=ACT.Sqrt
         )
-        nc.sync.dma_start(out=out_1.rearrange("(i p) -> i p", p=P), in_=l1_rows[0:ROW_TILES, :])
-        nc.sync.dma_start(out=out_0.rearrange("(i p) -> i p", p=P), in_=l2_rows[0:ROW_TILES, :])
+        split = ROW_TILES - 1
+        for queue, out, rows in ((nc.sync, out_1, l1_rows), (nc.scalar, out_0, l2_rows)):
+            out_tiles = out.rearrange("(i p) -> i p", p=P)
+            queue.dma_start(out=out_tiles[0:split, :], in_=rows[0:split, :])
+            queue.dma_start(out=out_tiles[split:ROW_TILES, :], in_=rows[split:ROW_TILES, :])

@@ -12,6 +12,7 @@ FP8X4 = mybir.dt.float8_e4m3fn_x4
 FP4X4 = mybir.dt.float4_e2m1fn_x4
 ACT = mybir.ActivationFunctionType
 ALU = mybir.AluOpType
+AX = mybir.AxisListType
 
 P = 128
 PACK = 4
@@ -99,10 +100,10 @@ def tile_nnapprox_pa_s_kernel(
         def load_rows(queue, x_sb, x_rows, first, end):
             queue.dma_start(out=x_sb[:, first:end, :], in_=x_rows[:, first:end, :])
 
-        load_plane(fc1_plane_in, fc1_w_scales, 1)
         load_rows(nc.sync, wk_sb, wk_rows, 0, 1)
-        load_rows(nc.sync, wk_sb, wk_rows, 1, 3)
+        load_plane(fc1_plane_in, fc1_w_scales, 1)
         load_words(fc1_words_in, fc1_w_words, 1)
+        load_rows(nc.sync, wk_sb, wk_rows, 1, 3)
         load_rows(nc.sync, wk_sb, wk_rows, 3, 5)
         nc.sync.dma_start(out=bias1[:], in_=fc1_b.rearrange("(p t) -> p t", t=PACK))
         load_rows(nc.sync, g0_sb, g0_rows, 0, 1)
@@ -253,58 +254,66 @@ def tile_nnapprox_pa_s_kernel(
                 out=sizes[i][:],
                 in_=diff[i][:],
                 func=ACT.Abs,
-                scale=1.0 / D,
                 accum_out=size_sums[:, i : i + 1],
             )
 
+        def sum_sizes_on_vector(i):
+            nc.vector.tensor_reduce(
+                out=size_sums[:, i : i + 1],
+                in_=diff[i][:],
+                axis=AX.X,
+                op=ALU.add,
+                apply_absolute_value=True,
+            )
+
+        regroup_fc1()
         turn_c(0)
         copy_c(0, nc.scalar.copy)
+        quantise_c(0)
         turn_c(1)
         copy_c(1, nc.scalar.copy)
-        quantise_c(0)
+        quantise_c(1)
         turn_c(2)
         copy_c(2, nc.scalar.copy)
-        quantise_c(1)
         turn_c(3)
-        copy_c(3, nc.scalar.copy)
-        regroup_fc1()
+        copy_c(3, nc.vector.tensor_copy)
         quantise_c(2)
         turn_c(4)
         copy_c(4, nc.scalar.copy)
         quantise_c(3)
         multiply_c(0)
-        silu(0)
         quantise_c(4)
         multiply_c(1)
+        silu(0)
+        multiply_c(2)
         silu(1)
         group_h(0)
-        multiply_c(2)
-        silu(2)
-        quantise_h(0)
-        group_h(1)
         multiply_c(3)
-        silu(3)
-        quantise_h(1)
-        group_h(2)
+        quantise_h(0)
         multiply_c(4)
-        silu(4)
         turn_g(0)
+        silu(2)
+        group_h(1)
         copy_g(0, nc.vector.tensor_copy)
-        nc.scalar.activation(out=warm[:, 1:2], in_=warm[:, 1:2], func=ACT.Sqrt)
-        quantise_h(2)
+        quantise_h(1)
         turn_g(1)
-        copy_g(1, nc.vector.tensor_copy)
-        group_h(3)
+        silu(3)
+        group_h(2)
         quantise_g(0)
+        copy_g(1, nc.vector.tensor_copy)
+        quantise_h(2)
+        silu(4)
         turn_g(2)
-        copy_g(2, nc.scalar.copy)
-        quantise_h(3)
-        group_h(4)
+        group_h(3)
         quantise_g(1)
+        nc.scalar.activation(out=warm[:, 1:2], in_=warm[:, 1:2], func=ACT.Sqrt)
         turn_g(3)
-        copy_g(3, nc.vector.tensor_copy)
+        quantise_h(3)
         turn_g(4)
-        copy_g(4, nc.scalar.copy)
+        group_h(4)
+        copy_g(2, nc.scalar.copy)
+        copy_g(3, nc.scalar.copy)
+        quantise_g(2)
         quantise_h(4)
         bias2 = keep.tile([P, D], F32)
         bias2_bank = psum.tile([P, D], F32, tag="bank")
@@ -312,7 +321,7 @@ def tile_nnapprox_pa_s_kernel(
             out=bias2_bank[:], lhsT=ones[:], rhs=bias2_rows[:], start=True, stop=True
         )
         nc.vector.tensor_copy(out=bias2[:], in_=bias2_bank[:])
-        quantise_g(2)
+        copy_g(4, nc.scalar.copy)
         multiply_out(0)
         quantise_g(3)
         subtract_bias(0)
@@ -331,9 +340,9 @@ def tile_nnapprox_pa_s_kernel(
         subtract_bias(3)
         multiply_out(4)
         sum_squares(3)
-        sum_sizes(3)
         subtract_bias(4)
-        sum_sizes(4)
+        sum_sizes_on_vector(3)
+        sum_sizes_on_vector(4)
         sum_squares(4)
 
         size_bank = psum.tile([P, P], F32, tag="bank")
@@ -342,7 +351,9 @@ def tile_nnapprox_pa_s_kernel(
         nc.tensor.transpose(out=square_bank[:], in_=square_sums[:], identity=ident[:])
         l1_rows = keep.tile([P, P], F32)
         l2_rows = keep.tile([P, P], F32)
-        nc.vector.tensor_copy(out=l1_rows[0:ROW_TILES, :], in_=size_bank[0:ROW_TILES, :])
+        nc.vector.tensor_scalar_mul(
+            out=l1_rows[0:ROW_TILES, :], in0=size_bank[0:ROW_TILES, :], scalar1=1.0 / D
+        )
         nc.scalar.activation(
             out=l2_rows[0:ROW_TILES, :], in_=square_bank[0:ROW_TILES, :], func=ACT.Sqrt
         )

@@ -100,13 +100,15 @@ def tile_nnapprox_pa_s_kernel(
         def load_rows(queue, x_sb, x_rows, first, end):
             queue.dma_start(out=x_sb[:, first:end, :], in_=x_rows[:, first:end, :])
 
+        ident = keep.tile([P, P], F32)
+        load_rows(nc.gpsimd, g0_sb, g0_rows, 0, 1)
+        make_identity(nc, ident[:])
         load_rows(nc.sync, wk_sb, wk_rows, 0, 1)
+        load_rows(nc.sync, wk_sb, wk_rows, 1, 3)
         load_plane(fc1_plane_in, fc1_w_scales, 1)
         load_words(fc1_words_in, fc1_w_words, 1)
-        load_rows(nc.sync, wk_sb, wk_rows, 1, 3)
         load_rows(nc.sync, wk_sb, wk_rows, 3, 5)
         nc.sync.dma_start(out=bias1[:], in_=fc1_b.rearrange("(p t) -> p t", t=PACK))
-        load_rows(nc.sync, g0_sb, g0_rows, 0, 1)
         nc.sync.dma_start(out=bias2_rows[0:1, :], in_=fc2_b.rearrange("(o d) -> o d", o=1))
         load_rows(nc.sync, g0_sb, g0_rows, 1, 3)
         load_rows(nc.sync, g0_sb, g0_rows, 3, 5)
@@ -114,8 +116,6 @@ def tile_nnapprox_pa_s_kernel(
         load_words(w2_words, w2_0_words, G0_PASSES)
         load_plane(fc2_plane, fc2_w_scales, 1)
         load_words(fc2_words, fc2_w_words, 1)
-        ident = keep.tile([P, P], F32)
-        make_identity(nc, ident[:])
 
         fc1_words = keep.tile([P, 2 * R], U8, align_bytes=64)
         fc1_plane = keep.tile([P, R], U8, align_bytes=64)
@@ -275,74 +275,74 @@ def tile_nnapprox_pa_s_kernel(
         quantise_c(1)
         turn_c(2)
         copy_c(2, nc.scalar.copy)
-        turn_c(3)
-        copy_c(3, nc.vector.tensor_copy)
         quantise_c(2)
+        turn_c(3)
+        copy_c(3, nc.scalar.copy)
         turn_c(4)
         copy_c(4, nc.scalar.copy)
-        quantise_c(3)
-        multiply_c(0)
-        quantise_c(4)
-        multiply_c(1)
-        silu(0)
-        multiply_c(2)
-        silu(1)
-        group_h(0)
-        multiply_c(3)
-        quantise_h(0)
-        multiply_c(4)
         turn_g(0)
-        silu(2)
-        group_h(1)
+        multiply_c(0)
+        quantise_c(3)
+        quantise_c(4)
         copy_g(0, nc.vector.tensor_copy)
-        quantise_h(1)
-        turn_g(1)
-        silu(3)
-        group_h(2)
-        quantise_g(0)
-        copy_g(1, nc.vector.tensor_copy)
-        quantise_h(2)
-        silu(4)
-        turn_g(2)
-        group_h(3)
-        quantise_g(1)
-        nc.scalar.activation(out=warm[:, 1:2], in_=warm[:, 1:2], func=ACT.Sqrt)
-        turn_g(3)
-        quantise_h(3)
-        turn_g(4)
-        group_h(4)
-        copy_g(2, nc.scalar.copy)
-        copy_g(3, nc.scalar.copy)
-        quantise_g(2)
-        quantise_h(4)
+        silu(0)
+        multiply_c(1)
         bias2 = keep.tile([P, D], F32)
         bias2_bank = psum.tile([P, D], F32, tag="bank")
         nc.tensor.matmul(
             out=bias2_bank[:], lhsT=ones[:], rhs=bias2_rows[:], start=True, stop=True
         )
         nc.vector.tensor_copy(out=bias2[:], in_=bias2_bank[:])
+        quantise_g(0)
+        multiply_c(2)
+        silu(1)
+        group_h(0)
+        turn_g(1)
+        multiply_c(3)
+        copy_g(1, nc.vector.tensor_copy)
+        multiply_c(4)
+        silu(2)
+        group_h(1)
+        quantise_h(0)
+        quantise_g(1)
+        quantise_h(1)
+        silu(3)
+        turn_g(2)
+        group_h(2)
+        silu(4)
+        group_h(3)
+        turn_g(3)
+        quantise_h(2)
+        copy_g(2, nc.scalar.copy)
+        group_h(4)
+        turn_g(4)
+        quantise_h(3)
+        copy_g(3, nc.scalar.copy)
+        quantise_g(2)
+        quantise_h(4)
         copy_g(4, nc.scalar.copy)
+        nc.scalar.activation(out=warm[:, 1:2], in_=warm[:, 1:2], func=ACT.Sqrt)
         multiply_out(0)
         quantise_g(3)
         subtract_bias(0)
         multiply_out(1)
-        sum_squares(0)
-        sum_sizes(0)
         quantise_g(4)
         subtract_bias(1)
         multiply_out(2)
-        sum_squares(1)
-        sum_sizes(1)
+        sum_sizes_on_vector(0)
         subtract_bias(2)
         multiply_out(3)
-        sum_squares(2)
-        sum_sizes(2)
+        sum_sizes_on_vector(1)
         subtract_bias(3)
         multiply_out(4)
-        sum_squares(3)
+        sum_sizes_on_vector(2)
         subtract_bias(4)
         sum_sizes_on_vector(3)
         sum_sizes_on_vector(4)
+        sum_squares(0)
+        sum_squares(1)
+        sum_squares(2)
+        sum_squares(3)
         sum_squares(4)
 
         size_bank = psum.tile([P, P], F32, tag="bank")

@@ -22,6 +22,7 @@ PAIRS = K_PASS // 2
 B, D, F, R = 640, 128, 1024, 512
 C = 512
 ROW_TILES = B // P
+BANK = 512
 G0_PASSES = F // K_PASS
 QUADRANTS = 4
 
@@ -46,7 +47,8 @@ def tile_nnapprox_pa_s_kernel(
     nc = tc.nc
     with ExitStack() as ctx:
         keep = ctx.enter_context(tc.tile_pool(name="keep", bufs=1))
-        psum = ctx.enter_context(tc.psum_pool(name="psum", bufs=8))
+        psum = ctx.enter_context(tc.psum_pool(name="psum", bufs=7))
+        spare = ctx.enter_context(tc.psum_pool(name="spare", bufs=1))
         ctx.enter_context(tc.manual_schedule())
 
         def one_per_row_tile(shape, dtype, name):
@@ -62,6 +64,8 @@ def tile_nnapprox_pa_s_kernel(
         nc.vector.memset(fc1_plane_in[:].bitcast(I32), 0)
         warm = keep.tile([P, 2], F32)
         nc.vector.memset(warm[:], 0.0)
+        idle = keep.tile([P, 4 * P], BF16)
+        nc.vector.memset(idle[:], 0.0)
         nc.scalar.activation(out=warm[:, 0:1], in_=warm[:, 0:1], func=ACT.Silu)
         nc.vector.memset(bias2_rows[:], 0.0)
         nc.vector.memset(fc2_plane[:].bitcast(I32), 0)
@@ -101,31 +105,30 @@ def tile_nnapprox_pa_s_kernel(
             queue.dma_start(out=x_sb[:, first:end, :], in_=x_rows[:, first:end, :])
 
         ident = keep.tile([P, P], F32)
-        load_rows(nc.gpsimd, g0_sb, g0_rows, 0, 1)
         make_identity(nc, ident[:])
-        load_rows(nc.sync, wk_sb, wk_rows, 0, 1)
-        load_rows(nc.sync, wk_sb, wk_rows, 1, 3)
+        load_rows(nc.sync, wk_sb, wk_rows, 0, 3)
         load_plane(fc1_plane_in, fc1_w_scales, 1)
         load_words(fc1_words_in, fc1_w_words, 1)
+        load_rows(nc.sync, g0_sb, g0_rows, 0, 1)
         load_rows(nc.sync, wk_sb, wk_rows, 3, 5)
         nc.sync.dma_start(out=bias1[:], in_=fc1_b.rearrange("(p t) -> p t", t=PACK))
         nc.sync.dma_start(out=bias2_rows[0:1, :], in_=fc2_b.rearrange("(o d) -> o d", o=1))
         load_rows(nc.sync, g0_sb, g0_rows, 1, 3)
-        load_rows(nc.sync, g0_sb, g0_rows, 3, 5)
         load_plane(w2_plane, w2_0_scales, G0_PASSES)
         load_words(w2_words, w2_0_words, G0_PASSES)
+        load_rows(nc.sync, g0_sb, g0_rows, 3, 5)
         load_plane(fc2_plane, fc2_w_scales, 1)
         load_words(fc2_words, fc2_w_words, 1)
 
         fc1_words = keep.tile([P, 2 * R], U8, align_bytes=64)
         fc1_plane = keep.tile([P, R], U8, align_bytes=64)
-        c_grouped = one_per_row_tile([P, PACK * P], BF16, "c_grouped")
-        c_codes = one_per_row_tile([P, P], U32, "c_codes")
-        c_plane = one_per_row_tile([P, P], U8, "c_plane")
-        h_sb = one_per_row_tile([P, PACK, P], BF16, "h_sb")
-        h_grouped = one_per_row_tile([P, PACK * P], BF16, "h_grouped")
-        h_codes = one_per_row_tile([P, P], U32, "h_codes")
-        h_plane = one_per_row_tile([P, P], U8, "h_plane")
+        c_grouped = keep.tile([P, PACK * B], BF16, align_bytes=64)
+        c_codes = keep.tile([P, B], U32, align_bytes=64)
+        c_plane = keep.tile([P, B], U8, align_bytes=64)
+        h_sb = keep.tile([P, PACK * B], BF16, align_bytes=64)
+        h_grouped = keep.tile([P, PACK * B], BF16, align_bytes=64)
+        h_codes = keep.tile([P, B], U32, align_bytes=64)
+        h_plane = keep.tile([P, B], U8, align_bytes=64)
         g_grouped = one_per_row_tile([P, G0_PASSES * PACK * P], BF16, "g_grouped")
         g_codes = one_per_row_tile([P, G0_PASSES * P], U32, "g_codes")
         g_plane = one_per_row_tile([P, G0_PASSES * P], U8, "g_plane")
@@ -134,26 +137,20 @@ def tile_nnapprox_pa_s_kernel(
         sizes = one_per_row_tile([P, D], F32, "sizes")
         banks = {}
 
-        def turn_rows(x, passes, key):
-            x_pairs = x.bitcast(F32)
-            turned = psum.tile([P, passes, 2, P], F32, tag="bank")
-            for g in range(passes):
-                for u in range(2):
-                    nc.tensor.transpose(
-                        out=turned[:, g, u, :],
-                        in_=x_pairs[:, PAIRS * g + u : PAIRS * (g + 1) : 2],
-                        identity=ident[:],
-                    )
-            banks[key] = turned
+        def turn_pass(x_pairs, turned):
+            for u in range(2):
+                nc.tensor.transpose(
+                    out=turned[:, u, :], in_=x_pairs[:, u:PAIRS:2], identity=ident[:]
+                )
 
-        def group_rows(copy_out, key, passes, grouped):
+        def pair_words(copy_out, turned, grouped):
             copy_out(
-                out=grouped[:].bitcast(F32).rearrange("p (g b u) -> p g b u", g=passes, u=2),
-                in_=banks[key][:].rearrange("p g u b -> p g b u"),
+                out=grouped.bitcast(F32).rearrange("p (n b u) -> p n b u", u=2, b=P),
+                in_=turned[:].rearrange("p n u b -> p n b u"),
             )
 
         def quantise(grouped, codes, plane):
-            nc.vector.quantize_mx(out=codes[:].bitcast(FP8X4), scales=plane[:], in_=grouped[:])
+            nc.vector.quantize_mx(out=codes.bitcast(FP8X4), scales=plane, in_=grouped)
 
         def regroup_fc1():
             nc.vector.tensor_copy(
@@ -165,56 +162,79 @@ def tile_nnapprox_pa_s_kernel(
                 in_=fc1_words_in[:].rearrange("p (m t e) -> p t m e", t=PACK, e=2),
             )
 
-        def turn_c(i):
-            turn_rows(wk_sb[:, i, :], 1, ("c", i))
+        def columns(tile, first, end, width):
+            return tile[:, width * first : width * end]
 
-        def copy_c(i, copy_out):
-            group_rows(copy_out, ("c", i), 1, c_grouped[i])
+        def turn_c(first, end):
+            turned = psum.tile([P, end - first, 2, P], F32, tag="bank")
+            for i in range(first, end):
+                turn_pass(wk_sb[:, i, :].bitcast(F32), turned[:, i - first, :, :])
+            banks[("c", first)] = turned
 
-        def quantise_c(i):
-            quantise(c_grouped[i], c_codes[i], c_plane[i])
+        def copy_c(first, end, copy_out):
+            pair_words(copy_out, banks[("c", first)], columns(c_grouped, first, end, PACK * P))
 
-        def multiply_c(i):
-            h_bank = psum.tile([P, PACK, P], F32, tag="bank")
+        def quantise_c(first, end):
+            quantise(
+                columns(c_grouped, first, end, PACK * P),
+                columns(c_codes, first, end, P),
+                columns(c_plane, first, end, P),
+            )
+
+        def multiply_c(first, end):
+            rows = P * (end - first)
+            in_bank = BANK // rows
             for t in range(PACK):
+                if t % in_bank == 0:
+                    h_bank = psum.tile([P, in_bank, rows], F32, tag="bank")
                 nc.tensor.matmul_mx(
-                    out=h_bank[:, t, :],
+                    out=h_bank[:, t % in_bank, :],
                     lhsT=fc1_words[:, 2 * P * t : 2 * P * (t + 1)].bitcast(FP4X4),
                     lhsT_scale=fc1_plane[:, P * t : P * (t + 1)],
-                    rhs=c_codes[i][:].bitcast(FP8X4),
-                    rhs_scale=c_plane[i][:],
+                    rhs=columns(c_codes, first, end, P).bitcast(FP8X4),
+                    rhs_scale=columns(c_plane, first, end, P),
                     start=True,
                     stop=True,
                 )
-            banks[("h", i)] = h_bank
+                banks[("h", first, t)] = h_bank[:, t % in_bank, :]
 
-        def silu(i):
+        def silu(first, end):
+            rows = P * (end - first)
             for t in range(PACK):
+                start = PACK * P * first + rows * t
                 nc.scalar.activation(
-                    out=h_sb[i][:, t, :],
-                    in_=banks[("h", i)][:, t, :],
+                    out=h_sb[:, start : start + rows],
+                    in_=banks[("h", first, t)],
                     func=ACT.Silu,
                     bias=bias1[:, t : t + 1],
                 )
 
-        def group_h(i):
+        def group_h(first, end):
             nc.vector.tensor_scalar_mul(
-                out=h_grouped[i][:].rearrange("p (b t) -> p b t", t=PACK),
-                in0=h_sb[i][:].rearrange("p t b -> p b t"),
+                out=columns(h_grouped, first, end, PACK * P).rearrange("p (b t) -> p b t", t=PACK),
+                in0=columns(h_sb, first, end, PACK * P).rearrange("p (t b) -> p b t", t=PACK),
                 scalar1=-1.0,
             )
 
-        def quantise_h(i):
-            quantise(h_grouped[i], h_codes[i], h_plane[i])
+        def quantise_h(first, end):
+            quantise(
+                columns(h_grouped, first, end, PACK * P),
+                columns(h_codes, first, end, P),
+                columns(h_plane, first, end, P),
+            )
 
         def turn_g(i):
-            turn_rows(g0_sb[:, i, :], G0_PASSES, ("g", i))
+            turned = psum.tile([P, G0_PASSES, 2, P], F32, tag="bank")
+            for g in range(G0_PASSES):
+                x_pairs = g0_sb[:, i, :].bitcast(F32)[:, PAIRS * g : PAIRS * (g + 1)]
+                turn_pass(x_pairs, turned[:, g, :, :])
+            banks[("g", i)] = turned
 
         def copy_g(i, copy_out):
-            group_rows(copy_out, ("g", i), G0_PASSES, g_grouped[i])
+            pair_words(copy_out, banks[("g", i)], g_grouped[i][:])
 
         def quantise_g(i):
-            quantise(g_grouped[i], g_codes[i], g_plane[i])
+            quantise(g_grouped[i][:], g_codes[i][:], g_plane[i][:])
 
         def multiply_out(i):
             out_bank = psum.tile([P, D], F32, tag="bank")
@@ -230,8 +250,8 @@ def tile_nnapprox_pa_s_kernel(
                 )
             nc.tensor.matmul_mx(
                 out=out_bank[:],
-                lhsT=h_codes[i][:].bitcast(FP8X4),
-                lhsT_scale=h_plane[i][:],
+                lhsT=columns(h_codes, i, i + 1, P).bitcast(FP8X4),
+                lhsT_scale=columns(h_plane, i, i + 1, P),
                 rhs=fc2_words[:].bitcast(FP4X4),
                 rhs_scale=fc2_plane[:],
                 start=False,
@@ -266,84 +286,85 @@ def tile_nnapprox_pa_s_kernel(
                 apply_absolute_value=True,
             )
 
+        idle_bank = spare.tile([P, 4 * P], F32, tag="spare")
+
+        def keep_busy(times):
+            for unused in range(times):
+                nc.tensor.matmul(
+                    out=idle_bank[:], lhsT=idle[:, 0:P], rhs=idle[:], start=True, stop=True
+                )
+
+        keep_busy(3)
+        turn_c(0, 1)
+        copy_c(0, 1, nc.scalar.copy)
         regroup_fc1()
-        turn_c(0)
-        copy_c(0, nc.scalar.copy)
-        quantise_c(0)
-        turn_c(1)
-        copy_c(1, nc.scalar.copy)
-        quantise_c(1)
-        turn_c(2)
-        copy_c(2, nc.scalar.copy)
-        quantise_c(2)
-        turn_c(3)
-        copy_c(3, nc.scalar.copy)
-        turn_c(4)
-        copy_c(4, nc.scalar.copy)
+        turn_c(1, 2)
+        copy_c(1, 2, nc.scalar.copy)
+        quantise_c(0, 1)
+        turn_c(2, 3)
+        copy_c(2, 3, nc.scalar.copy)
+        quantise_c(1, 2)
         turn_g(0)
-        multiply_c(0)
-        quantise_c(3)
-        quantise_c(4)
+        quantise_c(2, 3)
+        turn_c(3, 4)
+        copy_c(3, 4, nc.scalar.copy)
+        quantise_c(3, 4)
+        turn_c(4, 5)
+        copy_c(4, 5, nc.scalar.copy)
+        quantise_c(4, 5)
+        multiply_c(0, 1)
+        silu(0, 1)
         copy_g(0, nc.vector.tensor_copy)
-        silu(0)
-        multiply_c(1)
+        multiply_c(1, 3)
+        silu(1, 3)
+        quantise_g(0)
+        turn_g(1)
+        group_h(0, 1)
+        multiply_c(3, 5)
+        silu(3, 5)
+        copy_g(1, nc.vector.tensor_copy)
+        turn_g(2)
+        copy_g(2, nc.scalar.copy)
+        quantise_h(0, 1)
+        turn_g(3)
+        copy_g(3, nc.scalar.copy)
+        group_h(1, 3)
+        turn_g(4)
+        copy_g(4, nc.scalar.copy)
+        quantise_g(1)
         bias2 = keep.tile([P, D], F32)
         bias2_bank = psum.tile([P, D], F32, tag="bank")
         nc.tensor.matmul(
             out=bias2_bank[:], lhsT=ones[:], rhs=bias2_rows[:], start=True, stop=True
         )
-        nc.vector.tensor_copy(out=bias2[:], in_=bias2_bank[:])
-        quantise_g(0)
-        multiply_c(2)
-        silu(1)
-        group_h(0)
-        turn_g(1)
-        multiply_c(3)
-        copy_g(1, nc.vector.tensor_copy)
-        multiply_c(4)
-        silu(2)
-        group_h(1)
-        quantise_h(0)
-        quantise_g(1)
-        quantise_h(1)
-        silu(3)
-        turn_g(2)
-        group_h(2)
-        silu(4)
-        group_h(3)
-        turn_g(3)
-        quantise_h(2)
-        copy_g(2, nc.scalar.copy)
-        group_h(4)
-        turn_g(4)
-        quantise_h(3)
-        copy_g(3, nc.scalar.copy)
-        quantise_g(2)
-        quantise_h(4)
-        copy_g(4, nc.scalar.copy)
         nc.scalar.activation(out=warm[:, 1:2], in_=warm[:, 1:2], func=ACT.Sqrt)
+        quantise_h(1, 3)
         multiply_out(0)
-        quantise_g(3)
-        subtract_bias(0)
+        group_h(3, 5)
         multiply_out(1)
-        quantise_g(4)
-        subtract_bias(1)
+        quantise_g(2)
         multiply_out(2)
+        quantise_h(3, 5)
+        nc.vector.tensor_copy(out=bias2[:], in_=bias2_bank[:])
+        quantise_g(3)
+        multiply_out(3)
+        subtract_bias(0)
+        sum_squares(0)
+        quantise_g(4)
+        multiply_out(4)
+        subtract_bias(1)
+        sum_squares(1)
         sum_sizes_on_vector(0)
         subtract_bias(2)
-        multiply_out(3)
+        sum_squares(2)
         sum_sizes_on_vector(1)
         subtract_bias(3)
-        multiply_out(4)
+        sum_squares(3)
         sum_sizes_on_vector(2)
         subtract_bias(4)
+        sum_squares(4)
         sum_sizes_on_vector(3)
         sum_sizes_on_vector(4)
-        sum_squares(0)
-        sum_squares(1)
-        sum_squares(2)
-        sum_squares(3)
-        sum_squares(4)
 
         size_bank = psum.tile([P, P], F32, tag="bank")
         nc.tensor.transpose(out=size_bank[:], in_=size_sums[:], identity=ident[:])

@@ -64,7 +64,7 @@ def tile_nnapprox_pa_s_kernel(
         nc.vector.memset(fc1_plane_in[:].bitcast(I32), 0)
         warm = keep.tile([P, 2], F32)
         nc.vector.memset(warm[:], 0.0)
-        idle = keep.tile([P, 4 * P], BF16)
+        idle = keep.tile([P, 2 * P], F32)
         nc.vector.memset(idle[:], 0.0)
         nc.scalar.activation(out=warm[:, 0:1], in_=warm[:, 0:1], func=ACT.Silu)
         nc.vector.memset(bias2_rows[:], 0.0)
@@ -211,8 +211,12 @@ def tile_nnapprox_pa_s_kernel(
 
         def group_h(first, end):
             nc.vector.tensor_scalar_mul(
-                out=columns(h_grouped, first, end, PACK * P).rearrange("p (b t) -> p b t", t=PACK),
-                in0=columns(h_sb, first, end, PACK * P).rearrange("p (t b) -> p b t", t=PACK),
+                out=columns(h_grouped, first, end, PACK * P).rearrange(
+                    "p (c i t) -> p c t i", i=4, t=PACK
+                ),
+                in0=columns(h_sb, first, end, PACK * P).rearrange(
+                    "p (t c i) -> p c t i", i=4, t=PACK
+                ),
                 scalar1=-1.0,
             )
 
@@ -288,13 +292,18 @@ def tile_nnapprox_pa_s_kernel(
 
         idle_bank = spare.tile([P, 4 * P], F32, tag="spare")
 
-        def keep_busy(times):
-            for unused in range(times):
-                nc.tensor.matmul(
-                    out=idle_bank[:], lhsT=idle[:, 0:P], rhs=idle[:], start=True, stop=True
-                )
+        def keep_busy(columns, zeros):
+            nc.tensor.matmul(
+                out=idle_bank[:, 0:columns],
+                lhsT=zeros[:, 0:P],
+                rhs=zeros[:, 0:columns],
+                start=True,
+                stop=True,
+            )
 
-        keep_busy(3)
+        for unused in range(3):
+            keep_busy(4 * P, idle[:].bitcast(BF16))
+        keep_busy(P // 2, idle[:])
         turn_c(0, 1)
         copy_c(0, 1, nc.scalar.copy)
         regroup_fc1()
@@ -308,13 +317,13 @@ def tile_nnapprox_pa_s_kernel(
         quantise_c(2, 3)
         turn_c(3, 4)
         copy_c(3, 4, nc.scalar.copy)
+        copy_g(0, nc.vector.tensor_copy)
         quantise_c(3, 4)
         turn_c(4, 5)
         copy_c(4, 5, nc.scalar.copy)
         quantise_c(4, 5)
         multiply_c(0, 1)
         silu(0, 1)
-        copy_g(0, nc.vector.tensor_copy)
         multiply_c(1, 3)
         silu(1, 3)
         quantise_g(0)

@@ -47,8 +47,7 @@ def tile_nnapprox_pa_s_kernel(
     nc = tc.nc
     with ExitStack() as ctx:
         keep = ctx.enter_context(tc.tile_pool(name="keep", bufs=1))
-        psum = ctx.enter_context(tc.psum_pool(name="psum", bufs=7))
-        spare = ctx.enter_context(tc.psum_pool(name="spare", bufs=1))
+        psum = ctx.enter_context(tc.psum_pool(name="psum", bufs=8))
         ctx.enter_context(tc.manual_schedule())
 
         def one_per_row_tile(shape, dtype, name):
@@ -290,7 +289,7 @@ def tile_nnapprox_pa_s_kernel(
                 apply_absolute_value=True,
             )
 
-        idle_bank = spare.tile([P, 4 * P], F32, tag="spare")
+        idle_bank = psum.tile([P, 4 * P], F32, tag="bank")
 
         def keep_busy(columns, zeros):
             nc.tensor.matmul(
@@ -301,9 +300,9 @@ def tile_nnapprox_pa_s_kernel(
                 stop=True,
             )
 
+        keep_busy(3 * P // 4, idle[:])
         for unused in range(3):
             keep_busy(4 * P, idle[:].bitcast(BF16))
-        keep_busy(P // 2, idle[:])
         turn_c(0, 1)
         copy_c(0, 1, nc.scalar.copy)
         regroup_fc1()

from contextlib import ExitStack

import concourse.mybir as mybir
from concourse.masks import make_identity

F32 = mybir.dt.float32
BF16 = mybir.dt.bfloat16
I32 = mybir.dt.int32
U32 = mybir.dt.uint32
U8 = mybir.dt.uint8
FP8X4 = mybir.dt.float8_e4m3fn_x4
FP4X4 = mybir.dt.float4_e2m1fn_x4
ACT = mybir.ActivationFunctionType
ALU = mybir.AluOpType
AX = mybir.AxisListType

P = 128
PACK = 4
K_PASS = P * PACK
PAIRS = K_PASS // 2

B, D, F, R = 640, 128, 1024, 512
C = 512
ROW_TILES = B // P
BANK = 512
G0_PASSES = F // K_PASS
QUADRANTS = 4

FLOPS = 2 * B * (F * D + C * R + R * D)


def tile_nnapprox_pa_s_kernel(
    tc,
    g0,
    w2_0_words,
    w2_0_scales,
    wk_rest,
    fc1_w_words,
    fc1_w_scales,
    fc1_b,
    fc2_w_words,
    fc2_w_scales,
    fc2_b,
    out_0,
    out_1,
):
    nc = tc.nc
    with ExitStack() as ctx:
        keep = ctx.enter_context(tc.tile_pool(name="keep", bufs=1))
        psum = ctx.enter_context(tc.psum_pool(name="psum", bufs=8))
        ctx.enter_context(tc.manual_schedule())

        def one_per_row_tile(shape, dtype, name):
            return [
                keep.tile(shape, dtype, name="%s%d" % (name, i), align_bytes=64)
                for i in range(ROW_TILES)
            ]

        fc1_plane_in = keep.tile([P, R], U8, align_bytes=64)
        fc2_plane = keep.tile([P, D], U8, align_bytes=64)
        w2_plane = keep.tile([P, G0_PASSES * D], U8, align_bytes=64)
        bias2_rows = keep.tile([P, D], BF16)
        nc.vector.memset(fc1_plane_in[:].bitcast(I32), 0)
        warm = keep.tile([P, 2], F32)
        nc.vector.memset(warm[:], 0.0)
        idle = keep.tile([P, 2 * P], F32)
        nc.vector.memset(idle[:], 0.0)
        nc.scalar.activation(out=warm[:, 0:1], in_=warm[:, 0:1], func=ACT.Silu)
        nc.vector.memset(bias2_rows[:], 0.0)
        nc.vector.memset(fc2_plane[:].bitcast(I32), 0)
        nc.vector.memset(w2_plane[:].bitcast(I32), 0)
        ones = keep.tile([P, P], BF16)
        nc.vector.memset(ones[:], 1.0)
        square_sums = keep.tile([P, P], F32)
        nc.vector.memset(square_sums[:], 0.0)
        size_sums = keep.tile([P, P], F32)
        nc.vector.memset(size_sums[:], 0.0)

        wk_rows = wk_rest.rearrange("(i p) n d -> p i (n d)", p=P)
        g0_rows = g0.rearrange("(i p) k -> p i k", p=P)
        wk_sb = keep.tile([P, ROW_TILES, C], BF16, align_bytes=64)
        g0_sb = keep.tile([P, ROW_TILES, F], BF16, align_bytes=64)
        fc1_words_in = keep.tile([P, 2 * R], U8, align_bytes=64)
        fc2_words = keep.tile([P, 2 * D], U8, align_bytes=64)
        w2_words = keep.tile([P, G0_PASSES * 2 * D], U8, align_bytes=64)
        bias1 = keep.tile([P, PACK], BF16)

        def load_plane(plane, scales, passes):
            for q4 in range(QUADRANTS):
                nc.sync.dma_start(
                    out=plane[32 * q4 : 32 * q4 + 4, :]
                    .bitcast(I32)
                    .rearrange("r (g w) -> r g w", g=passes),
                    in_=scales[:, 4 * q4 : 4 * q4 + 4, :].bitcast(I32).rearrange("g r w -> r g w"),
                )

        def load_words(words, packed, passes):
            nc.sync.dma_start(
                out=words[:].bitcast(I32).rearrange("p (g w) -> p g w", g=passes),
                in_=packed.bitcast(I32).rearrange("g p w -> p g w"),
            )

        def load_rows(queue, x_sb, x_rows, first, end):
            queue.dma_start(out=x_sb[:, first:end, :], in_=x_rows[:, first:end, :])

        ident = keep.tile([P, P], F32)
        make_identity(nc, ident[:])
        load_rows(nc.sync, wk_sb, wk_rows, 0, 3)
        load_plane(fc1_plane_in, fc1_w_scales, 1)
        load_words(fc1_words_in, fc1_w_words, 1)
        load_rows(nc.sync, g0_sb, g0_rows, 0, 1)
        load_rows(nc.sync, wk_sb, wk_rows, 3, 5)
        nc.sync.dma_start(out=bias1[:], in_=fc1_b.rearrange("(p t) -> p t", t=PACK))
        nc.sync.dma_start(out=bias2_rows[0:1, :], in_=fc2_b.rearrange("(o d) -> o d", o=1))
        load_rows(nc.sync, g0_sb, g0_rows, 1, 3)
        load_plane(w2_plane, w2_0_scales, G0_PASSES)
        load_words(w2_words, w2_0_words, G0_PASSES)
        load_rows(nc.sync, g0_sb, g0_rows, 3, 5)
        load_plane(fc2_plane, fc2_w_scales, 1)
        load_words(fc2_words, fc2_w_words, 1)

        fc1_words = keep.tile([P, 2 * R], U8, align_bytes=64)
        fc1_plane = keep.tile([P, R], U8, align_bytes=64)
        c_grouped = keep.tile([P, PACK * B], BF16, align_bytes=64)
        c_codes = keep.tile([P, B], U32, align_bytes=64)
        c_plane = keep.tile([P, B], U8, align_bytes=64)
        h_sb = keep.tile([P, PACK * B], BF16, align_bytes=64)
        h_grouped = keep.tile([P, PACK * B], BF16, align_bytes=64)
        h_codes = keep.tile([P, B], U32, align_bytes=64)
        h_plane = keep.tile([P, B], U8, align_bytes=64)
        g_grouped = one_per_row_tile([P, G0_PASSES * PACK * P], BF16, "g_grouped")
        g_codes = one_per_row_tile([P, G0_PASSES * P], U32, "g_codes")
        g_plane = one_per_row_tile([P, G0_PASSES * P], U8, "g_plane")
        diff = one_per_row_tile([P, D], F32, "diff")
        squares = one_per_row_tile([P, D], F32, "squares")
        sizes = one_per_row_tile([P, D], F32, "sizes")
        banks = {}

        def turn_pass(x_pairs, turned):
            for u in range(2):
                nc.tensor.transpose(
                    out=turned[:, u, :], in_=x_pairs[:, u:PAIRS:2], identity=ident[:]
                )

        def pair_words(copy_out, turned, grouped):
            copy_out(
                out=grouped.bitcast(F32).rearrange("p (n b u) -> p n b u", u=2, b=P),
                in_=turned[:].rearrange("p n u b -> p n b u"),
            )

        def quantise(grouped, codes, plane):
            nc.vector.quantize_mx(out=codes.bitcast(FP8X4), scales=plane, in_=grouped)

        def regroup_fc1():
            nc.vector.tensor_copy(
                out=fc1_plane[:].rearrange("p (t m) -> p t m", t=PACK),
                in_=fc1_plane_in[:].rearrange("p (m t) -> p t m", t=PACK),
            )
            nc.vector.tensor_copy(
                out=fc1_words[:].rearrange("p (t m e) -> p t m e", t=PACK, e=2),
                in_=fc1_words_in[:].rearrange("p (m t e) -> p t m e", t=PACK, e=2),
            )

        def columns(tile, first, end, width):
            return tile[:, width * first : width * end]

        def turn_c(first, end):
            turned = psum.tile([P, end - first, 2, P], F32, tag="bank")
            for i in range(first, end):
                turn_pass(wk_sb[:, i, :].bitcast(F32), turned[:, i - first, :, :])
            banks[("c", first)] = turned

        def copy_c(first, end, copy_out):
            pair_words(copy_out, banks[("c", first)], columns(c_grouped, first, end, PACK * P))

        def quantise_c(first, end):
            quantise(
                columns(c_grouped, first, end, PACK * P),
                columns(c_codes, first, end, P),
                columns(c_plane, first, end, P),
            )

        def multiply_c(first, end):
            rows = P * (end - first)
            in_bank = BANK // rows
            for t in range(PACK):
                if t % in_bank == 0:
                    h_bank = psum.tile([P, in_bank, rows], F32, tag="bank")
                nc.tensor.matmul_mx(
                    out=h_bank[:, t % in_bank, :],
                    lhsT=fc1_words[:, 2 * P * t : 2 * P * (t + 1)].bitcast(FP4X4),
                    lhsT_scale=fc1_plane[:, P * t : P * (t + 1)],
                    rhs=columns(c_codes, first, end, P).bitcast(FP8X4),
                    rhs_scale=columns(c_plane, first, end, P),
                    start=True,
                    stop=True,
                )
                banks[("h", first, t)] = h_bank[:, t % in_bank, :]

        def silu(first, end):
            rows = P * (end - first)
            for t in range(PACK):
                start = PACK * P * first + rows * t
                nc.scalar.activation(
                    out=h_sb[:, start : start + rows],
                    in_=banks[("h", first, t)],
                    func=ACT.Silu,
                    bias=bias1[:, t : t + 1],
                )

        def group_h(first, end):
            nc.vector.tensor_scalar_mul(
                out=columns(h_grouped, first, end, PACK * P).rearrange(
                    "p (c i t) -> p c t i", i=4, t=PACK
                ),
                in0=columns(h_sb, first, end, PACK * P).rearrange(
                    "p (t c i) -> p c t i", i=4, t=PACK
                ),
                scalar1=-1.0,
            )

        def quantise_h(first, end):
            quantise(
                columns(h_grouped, first, end, PACK * P),
                columns(h_codes, first, end, P),
                columns(h_plane, first, end, P),
            )

        def turn_g(i):
            turned = psum.tile([P, G0_PASSES, 2, P], F32, tag="bank")
            for g in range(G0_PASSES):
                x_pairs = g0_sb[:, i, :].bitcast(F32)[:, PAIRS * g : PAIRS * (g + 1)]
                turn_pass(x_pairs, turned[:, g, :, :])
            banks[("g", i)] = turned

        def copy_g(i, copy_out):
            pair_words(copy_out, banks[("g", i)], g_grouped[i][:])

        def quantise_g(i):
            quantise(g_grouped[i][:], g_codes[i][:], g_plane[i][:])

        def multiply_out(i):
            out_bank = psum.tile([P, D], F32, tag="bank")
            for g in range(G0_PASSES):
                nc.tensor.matmul_mx(
                    out=out_bank[:],
                    lhsT=g_codes[i][:, P * g : P * (g + 1)].bitcast(FP8X4),
                    lhsT_scale=g_plane[i][:, P * g : P * (g + 1)],
                    rhs=w2_words[:, 2 * D * g : 2 * D * (g + 1)].bitcast(FP4X4),
                    rhs_scale=w2_plane[:, D * g : D * (g + 1)],
                    start=(g == 0),
                    stop=False,
                )
            nc.tensor.matmul_mx(
                out=out_bank[:],
                lhsT=columns(h_codes, i, i + 1, P).bitcast(FP8X4),
                lhsT_scale=columns(h_plane, i, i + 1, P),
                rhs=fc2_words[:].bitcast(FP4X4),
                rhs_scale=fc2_plane[:],
                start=False,
                stop=True,
            )
            banks[("out", i)] = out_bank

        def subtract_bias(i):
            nc.vector.tensor_tensor(
                out=diff[i][:], in0=banks[("out", i)][:], in1=bias2[:], op=ALU.subtract
            )

        def sum_squares(i):
            nc.scalar.activation(
                out=squares[i][:], in_=diff[i][:], func=ACT.Square, accum_out=square_sums[:, i : i + 1]
            )

        def sum_sizes(i):
            nc.scalar.activation(
                out=sizes[i][:],
                in_=diff[i][:],
                func=ACT.Abs,
                accum_out=size_sums[:, i : i + 1],
            )

        def sum_sizes_on_vector(i):
            nc.vector.tensor_reduce(
                out=size_sums[:, i : i + 1],
                in_=diff[i][:],
                axis=AX.X,
                op=ALU.add,
                apply_absolute_value=True,
            )

        idle_bank = psum.tile([P, 4 * P], F32, tag="bank")

        def keep_busy(columns, zeros):
            nc.tensor.matmul(
                out=idle_bank[:, 0:columns],
                lhsT=zeros[:, 0:P],
                rhs=zeros[:, 0:columns],
                start=True,
                stop=True,
            )

        keep_busy(3 * P // 4, idle[:])
        for unused in range(3):
            keep_busy(4 * P, idle[:].bitcast(BF16))
        turn_c(0, 1)
        copy_c(0, 1, nc.scalar.copy)
        regroup_fc1()
        turn_c(1, 2)
        copy_c(1, 2, nc.scalar.copy)
        quantise_c(0, 1)
        turn_c(2, 3)
        copy_c(2, 3, nc.scalar.copy)
        quantise_c(1, 2)
        turn_g(0)
        quantise_c(2, 3)
        turn_c(3, 4)
        copy_c(3, 4, nc.scalar.copy)
        copy_g(0, nc.vector.tensor_copy)
        quantise_c(3, 4)
        turn_c(4, 5)
        copy_c(4, 5, nc.scalar.copy)
        quantise_c(4, 5)
        multiply_c(0, 1)
        silu(0, 1)
        multiply_c(1, 3)
        silu(1, 3)
        quantise_g(0)
        turn_g(1)
        group_h(0, 1)
        multiply_c(3, 5)
        silu(3, 5)
        copy_g(1, nc.vector.tensor_copy)
        turn_g(2)
        copy_g(2, nc.scalar.copy)
        quantise_h(0, 1)
        turn_g(3)
        copy_g(3, nc.scalar.copy)
        group_h(1, 3)
        turn_g(4)
        copy_g(4, nc.scalar.copy)
        quantise_g(1)
        bias2 = keep.tile([P, D], F32)
        bias2_bank = psum.tile([P, D], F32, tag="bank")
        nc.tensor.matmul(
            out=bias2_bank[:], lhsT=ones[:], rhs=bias2_rows[:], start=True, stop=True
        )
        nc.scalar.activation(out=warm[:, 1:2], in_=warm[:, 1:2], func=ACT.Sqrt)
        quantise_h(1, 3)
        multiply_out(0)
        group_h(3, 5)
        multiply_out(1)
        quantise_g(2)
        multiply_out(2)
        quantise_h(3, 5)
        nc.vector.tensor_copy(out=bias2[:], in_=bias2_bank[:])
        quantise_g(3)
        multiply_out(3)
        subtract_bias(0)
        sum_squares(0)
        quantise_g(4)
        multiply_out(4)
        subtract_bias(1)
        sum_squares(1)
        sum_sizes_on_vector(0)
        subtract_bias(2)
        sum_squares(2)
        sum_sizes_on_vector(1)
        subtract_bias(3)
        sum_squares(3)
        sum_sizes_on_vector(2)
        subtract_bias(4)
        sum_squares(4)
        sum_sizes_on_vector(3)
        sum_sizes_on_vector(4)

        size_bank = psum.tile([P, P], F32, tag="bank")
        nc.tensor.transpose(out=size_bank[:], in_=size_sums[:], identity=ident[:])
        square_bank = psum.tile([P, P], F32, tag="bank")
        nc.tensor.transpose(out=square_bank[:], in_=square_sums[:], identity=ident[:])
        l1_rows = keep.tile([P, P], F32)
        l2_rows = keep.tile([P, P], F32)
        nc.vector.tensor_scalar_mul(
            out=l1_rows[0:ROW_TILES, :], in0=size_bank[0:ROW_TILES, :], scalar1=1.0 / D
        )
        nc.scalar.activation(
            out=l2_rows[0:ROW_TILES, :], in_=square_bank[0:ROW_TILES, :], func=ACT.Sqrt
        )
        split = ROW_TILES - 1
        for queue, out, rows in ((nc.sync, out_1, l1_rows), (nc.scalar, out_0, l2_rows)):
            out_tiles = out.rearrange("(i p) -> i p", p=P)
            queue.dma_start(out=out_tiles[0:split, :], in_=rows[0:split, :])
            queue.dma_start(out=out_tiles[split:ROW_TILES, :], in_=rows[split:ROW_TILES, :])
